import numpy as np
import ml_dtypes

BF16 = ml_dtypes.bfloat16


def bf(x):
    return np.asarray(x, np.float32).astype(BF16)


def f32(x):
    return np.asarray(x, np.float32)


def f64(x):
    return np.asarray(x).astype(np.float64)


def striped(idx):
    return np.tile(idx.reshape(-1, 16).T, (8, 1))


C, S, N, HEADS, SP, D, R = 512, 512, 256, 2, 128, 256, 8
SIGMA = 0.75


def setup_inputs():
    u = np.random.standard_normal((D, R)) / np.sqrt(D * R)
    return {"base": f32(np.random.standard_normal((C, S))), "spb": bf(0.8 * SP ** -0.25 * np.random.standard_normal((SP, C))), "h_feat": bf(u @ np.random.standard_normal((R, N))), "m_feat": bf(u @ np.random.standard_normal((R, N))), "offs": striped(np.random.permutation(S)[:N])}


def reference(base, spb, h_feat, m_feat, offs):
    idx = offs[:16].T.reshape(-1)
    e, hf, mf = f64(spb), f64(h_feat), f64(m_feat)
    d2 = np.sum(hf * hf, axis=0)[:, None] + np.sum(mf * mf, axis=0)[None, :] - 2.0 * (hf.T @ mf)
    kern = np.exp(-d2 / (2.0 * SIGMA ** 2))
    out = f64(base).copy()
    for h in range(HEADS):
        eh = e[:, h * N:(h + 1) * N]
        out[h * N:(h + 1) * N, idx] = eh.T @ eh + kern
    return out

@@ -1,0 +1,78 @@
+import concourse.mybir as mybir
+
+P = 128
+NODES = 256
+HEADS = 2
+SLOTS = 512
+FEATURES = 256
+SPATIAL = 128
+SIGMA = 0.75
+
+FEATURE_BLOCKS = FEATURES // P
+NODE_BLOCKS = NODES // P
+
+FLOPS = 2 * HEADS * NODES * NODES * SPATIAL + 2 * NODES * NODES * FEATURES
+
+BF16, F32, U16 = mybir.dt.bfloat16, mybir.dt.float32, mybir.dt.uint16
+ADD, MULT = mybir.AluOpType.add, mybir.AluOpType.mult
+EXP, COPY = mybir.ActivationFunctionType.Exp, mybir.ActivationFunctionType.Copy
+
+
+def tile_graphattnbias_kernel(tc, base, spb, h_feat, m_feat, offs, out):
+    nc = tc.nc
+    with (
+        tc.tile_pool(name="held", bufs=1) as held,
+        tc.psum_pool(name="psum", bufs=1) as psum,
+    ):
+        offsets = held.tile([P, NODES // 16], U16, name="offsets")
+        nc.sync.dma_start(offsets[:], offs)
+
+        h_sb = held.tile([P, FEATURE_BLOCKS, NODES], BF16, name="h_sb")
+        m_sb = held.tile([P, FEATURE_BLOCKS, NODES], BF16, name="m_sb")
+        nc.sync.dma_start(h_sb[:], h_feat.rearrange("(k p) n -> p k n", p=P))
+        nc.scalar.dma_start(m_sb[:], m_feat.rearrange("(k p) n -> p k n", p=P))
+
+        spb_sb = held.tile([SPATIAL, HEADS * NODES], BF16, name="spb_sb")
+        nc.scalar.dma_start(spb_sb[:], spb)
+
+        row_blocks = [(h, b) for b in range(NODE_BLOCKS) for h in range(HEADS)]
+        windows = {}
+        for i, (h, b) in enumerate(row_blocks):
+            row = h * NODES + b * P
+            windows[h, b] = held.tile([P, SLOTS], F32, name=f"window_{h}_{b}")
+            queue = nc.sync if i % 2 == 0 else nc.scalar
+            queue.dma_start(windows[h, b][:], base[row : row + P, :])
+
+        neg_half = held.tile([P, NODES], BF16, name="neg_half")
+        nc.gpsimd.memset(neg_half[:], -0.5)
+        h_sq = held.tile([P, FEATURE_BLOCKS, NODES], BF16, name="h_sq")
+        m_sq = held.tile([P, FEATURE_BLOCKS, NODES], BF16, name="m_sq")
+        nc.vector.tensor_tensor(h_sq[:], h_sb[:], h_sb[:], MULT)
+        nc.vector.tensor_tensor(m_sq[:], m_sb[:], m_sb[:], MULT)
+
+        kern = {}
+        for b in range(NODE_BLOCKS):
+            nodes_b = slice(b * P, (b + 1) * P)
+            neg_half_d2 = psum.tile([P, NODES], F32, name=f"neg_half_d2_{b}")
+            for k in range(FEATURE_BLOCKS):
+                nc.tensor.matmul(neg_half_d2[:], h_sb[:, k, nodes_b], m_sb[:, k, :], start=(k == 0), stop=False)
+            for k in range(FEATURE_BLOCKS):
+                nc.tensor.matmul(neg_half_d2[:], h_sq[:, k, nodes_b], neg_half[:], start=False, stop=False)
+            for k in range(FEATURE_BLOCKS):
+                nc.tensor.matmul(
+                    neg_half_d2[:], neg_half[:, 0:P], m_sq[:, k, :], start=False, stop=(k == FEATURE_BLOCKS - 1)
+                )
+            kern[b] = held.tile([P, NODES], F32, name=f"kern_{b}")
+            nc.scalar.activation(kern[b][:], neg_half_d2[:], EXP, scale=1.0 / SIGMA**2)
+
+        for i, (h, b) in enumerate(row_blocks):
+            row = h * NODES + b * P
+            gram = psum.tile([P, NODES], F32, name=f"gram_{h}_{b}")
+            nc.tensor.matmul(
+                gram[:], spb_sb[:, row : row + P], spb_sb[:, h * NODES : (h + 1) * NODES], start=True, stop=True
+            )
+            spatial = held.tile([P, NODES], F32, name=f"spatial_{h}_{b}")
+            nc.scalar.activation(spatial[:], gram[:], COPY)
+            nc.vector.tensor_tensor(windows[h, b][:].indirect(offsets[:]), spatial[:], kern[b][:], ADD)
+            queue = nc.sync if i % 2 == 0 else nc.scalar
+            queue.dma_start(out[row : row + P, :], windows[h, b][:])

@@ -24,9 +24,6 @@ def tile_graphattnbias_kernel(tc, base, spb, h_feat, m_feat, offs, out):
         tc.tile_pool(name="held", bufs=1) as held,
         tc.psum_pool(name="psum", bufs=1) as psum,
     ):
-        offsets = held.tile([P, NODES // 16], U16, name="offsets")
-        nc.sync.dma_start(offsets[:], offs)
-
         h_sb = held.tile([P, FEATURE_BLOCKS, NODES], BF16, name="h_sb")
         m_sb = held.tile([P, FEATURE_BLOCKS, NODES], BF16, name="m_sb")
         nc.sync.dma_start(h_sb[:], h_feat.rearrange("(k p) n -> p k n", p=P))
@@ -35,13 +32,15 @@ def tile_graphattnbias_kernel(tc, base, spb, h_feat, m_feat, offs, out):
         spb_sb = held.tile([SPATIAL, HEADS * NODES], BF16, name="spb_sb")
         nc.scalar.dma_start(spb_sb[:], spb)
 
-        row_blocks = [(h, b) for b in range(NODE_BLOCKS) for h in range(HEADS)]
+        offsets = held.tile([P, NODES // 16], U16, name="offsets")
+        nc.sync.dma_start(offsets[:], offs)
+
         windows = {}
-        for i, (h, b) in enumerate(row_blocks):
-            row = h * NODES + b * P
-            windows[h, b] = held.tile([P, SLOTS], F32, name=f"window_{h}_{b}")
-            queue = nc.sync if i % 2 == 0 else nc.scalar
-            queue.dma_start(windows[h, b][:], base[row : row + P, :])
+        for b in range(NODE_BLOCKS):
+            for h in range(HEADS):
+                row = h * NODES + b * P
+                windows[h, b] = held.tile([P, SLOTS], F32, name=f"window_{h}_{b}")
+                nc.sync.dma_start(windows[h, b][:], base[row : row + P, :])
 
         neg_half = held.tile([P, NODES], BF16, name="neg_half")
         nc.gpsimd.memset(neg_half[:], -0.5)
@@ -50,22 +49,7 @@ def tile_graphattnbias_kernel(tc, base, spb, h_feat, m_feat, offs, out):
         nc.vector.tensor_tensor(h_sq[:], h_sb[:], h_sb[:], MULT)
         nc.vector.tensor_tensor(m_sq[:], m_sb[:], m_sb[:], MULT)
 
-        kern = {}
-        for b in range(NODE_BLOCKS):
-            nodes_b = slice(b * P, (b + 1) * P)
-            neg_half_d2 = psum.tile([P, NODES], F32, name=f"neg_half_d2_{b}")
-            for k in range(FEATURE_BLOCKS):
-                nc.tensor.matmul(neg_half_d2[:], h_sb[:, k, nodes_b], m_sb[:, k, :], start=(k == 0), stop=False)
-            for k in range(FEATURE_BLOCKS):
-                nc.tensor.matmul(neg_half_d2[:], h_sq[:, k, nodes_b], neg_half[:], start=False, stop=False)
-            for k in range(FEATURE_BLOCKS):
-                nc.tensor.matmul(
-                    neg_half_d2[:], neg_half[:, 0:P], m_sq[:, k, :], start=False, stop=(k == FEATURE_BLOCKS - 1)
-                )
-            kern[b] = held.tile([P, NODES], F32, name=f"kern_{b}")
-            nc.scalar.activation(kern[b][:], neg_half_d2[:], EXP, scale=1.0 / SIGMA**2)
-
-        for i, (h, b) in enumerate(row_blocks):
+        def spatial_term(h, b):
             row = h * NODES + b * P
             gram = psum.tile([P, NODES], F32, name=f"gram_{h}_{b}")
             nc.tensor.matmul(
@@ -73,6 +57,26 @@ def tile_graphattnbias_kernel(tc, base, spb, h_feat, m_feat, offs, out):
             )
             spatial = held.tile([P, NODES], F32, name=f"spatial_{h}_{b}")
             nc.scalar.activation(spatial[:], gram[:], COPY)
-            nc.vector.tensor_tensor(windows[h, b][:].indirect(offsets[:]), spatial[:], kern[b][:], ADD)
-            queue = nc.sync if i % 2 == 0 else nc.scalar
-            queue.dma_start(out[row : row + P, :], windows[h, b][:])
+            return spatial
+
+        for b in range(NODE_BLOCKS):
+            nodes_b = slice(b * P, (b + 1) * P)
+
+            neg_half_d2 = psum.tile([P, NODES], F32, name=f"neg_half_d2_{b}")
+            for k in range(FEATURE_BLOCKS):
+                nc.tensor.matmul(neg_half_d2[:], h_sb[:, k, nodes_b], m_sb[:, k, :], start=(k == 0), stop=False)
+            spatial = {0: spatial_term(0, b)}
+            for k in range(FEATURE_BLOCKS):
+                nc.tensor.matmul(neg_half_d2[:], h_sq[:, k, nodes_b], neg_half[:], start=False, stop=False)
+            for k in range(FEATURE_BLOCKS):
+                nc.tensor.matmul(
+                    neg_half_d2[:], neg_half[:, 0:P], m_sq[:, k, :], start=False, stop=(k == FEATURE_BLOCKS - 1)
+                )
+            kern = held.tile([P, NODES], F32, name=f"kern_{b}")
+            nc.scalar.activation(kern[:], neg_half_d2[:], EXP, scale=1.0 / SIGMA**2)
+            spatial[1] = spatial_term(1, b)
+
+            for h in range(HEADS):
+                row = h * NODES + b * P
+                nc.vector.tensor_tensor(windows[h, b][:].indirect(offsets[:]), spatial[h][:], kern[:], ADD)
+                nc.sync.dma_start(out[row : row + P, :], windows[h, b][:])

@@ -42,6 +42,10 @@ def tile_graphattnbias_kernel(tc, base, spb, h_feat, m_feat, offs, out):
                 windows[h, b] = held.tile([P, SLOTS], F32, name=f"window_{h}_{b}")
                 nc.sync.dma_start(windows[h, b][:], base[row : row + P, :])
 
+        table_warmer = held.tile([P, 1], F32, name="table_warmer")
+        nc.vector.memset(table_warmer[:], 0.0)
+        nc.scalar.activation(table_warmer[:], table_warmer[:], EXP)
+
         neg_half = held.tile([P, NODES], BF16, name="neg_half")
         nc.gpsimd.memset(neg_half[:], -0.5)
         h_sq = held.tile([P, FEATURE_BLOCKS, NODES], BF16, name="h_sq")

@@ -42,10 +42,6 @@ def tile_graphattnbias_kernel(tc, base, spb, h_feat, m_feat, offs, out):
                 windows[h, b] = held.tile([P, SLOTS], F32, name=f"window_{h}_{b}")
                 nc.sync.dma_start(windows[h, b][:], base[row : row + P, :])
 
-        table_warmer = held.tile([P, 1], F32, name="table_warmer")
-        nc.vector.memset(table_warmer[:], 0.0)
-        nc.scalar.activation(table_warmer[:], table_warmer[:], EXP)
-
         neg_half = held.tile([P, NODES], BF16, name="neg_half")
         nc.gpsimd.memset(neg_half[:], -0.5)
         h_sq = held.tile([P, FEATURE_BLOCKS, NODES], BF16, name="h_sq")
@@ -55,7 +51,7 @@ def tile_graphattnbias_kernel(tc, base, spb, h_feat, m_feat, offs, out):
 
         def spatial_term(h, b):
             row = h * NODES + b * P
-            gram = psum.tile([P, NODES], F32, name=f"gram_{h}_{b}")
+            gram = psum.tile([P, NODES], F32, name=f"gram_{h}")
             nc.tensor.matmul(
                 gram[:], spb_sb[:, row : row + P], spb_sb[:, h * NODES : (h + 1) * NODES], start=True, stop=True
             )
@@ -66,7 +62,7 @@ def tile_graphattnbias_kernel(tc, base, spb, h_feat, m_feat, offs, out):
         for b in range(NODE_BLOCKS):
             nodes_b = slice(b * P, (b + 1) * P)
 
-            neg_half_d2 = psum.tile([P, NODES], F32, name=f"neg_half_d2_{b}")
+            neg_half_d2 = psum.tile([P, NODES], F32, name="neg_half_d2")
             for k in range(FEATURE_BLOCKS):
                 nc.tensor.matmul(neg_half_d2[:], h_sb[:, k, nodes_b], m_sb[:, k, :], start=(k == 0), stop=False)
             spatial = {0: spatial_term(0, b)}

@@ -11,6 +11,8 @@ SIGMA = 0.75
 FEATURE_BLOCKS = FEATURES // P
 NODE_BLOCKS = NODES // P
 
+WARMING_MATMULS = 8
+
 FLOPS = 2 * HEADS * NODES * NODES * SPATIAL + 2 * NODES * NODES * FEATURES
 
 BF16, F32, U16 = mybir.dt.bfloat16, mybir.dt.float32, mybir.dt.uint16
@@ -44,6 +46,11 @@ def tile_graphattnbias_kernel(tc, base, spb, h_feat, m_feat, offs, out):
 
         neg_half = held.tile([P, NODES], BF16, name="neg_half")
         nc.gpsimd.memset(neg_half[:], -0.5)
+
+        clock_warmer = psum.tile([P, NODES], F32, name="clock_warmer")
+        for i in range(WARMING_MATMULS):
+            nc.tensor.matmul(clock_warmer[:], neg_half[:, 0:P], neg_half[:], start=True, stop=True)
+
         h_sq = held.tile([P, FEATURE_BLOCKS, NODES], BF16, name="h_sq")
         m_sq = held.tile([P, FEATURE_BLOCKS, NODES], BF16, name="m_sq")
         nc.vector.tensor_tensor(h_sq[:], h_sb[:], h_sb[:], MULT)

@@ -28,8 +28,8 @@ def tile_graphattnbias_kernel(tc, base, spb, h_feat, m_feat, offs, out):
     ):
         h_sb = held.tile([P, FEATURE_BLOCKS, NODES], BF16, name="h_sb")
         m_sb = held.tile([P, FEATURE_BLOCKS, NODES], BF16, name="m_sb")
-        nc.sync.dma_start(h_sb[:], h_feat.rearrange("(k p) n -> p k n", p=P))
-        nc.scalar.dma_start(m_sb[:], m_feat.rearrange("(k p) n -> p k n", p=P))
+        nc.sync.dma_start(h_sb[:], h_feat.rearrange("(p k) n -> p k n", p=P))
+        nc.scalar.dma_start(m_sb[:], m_feat.rearrange("(p k) n -> p k n", p=P))
 
         spb_sb = held.tile([SPATIAL, HEADS * NODES], BF16, name="spb_sb")
         nc.scalar.dma_start(spb_sb[:], spb)

@@ -45,7 +45,7 @@ def tile_graphattnbias_kernel(tc, base, spb, h_feat, m_feat, offs, out):
                 nc.sync.dma_start(windows[h, b][:], base[row : row + P, :])
 
         neg_half = held.tile([P, NODES], BF16, name="neg_half")
-        nc.gpsimd.memset(neg_half[:], -0.5)
+        nc.vector.memset(neg_half[:], -0.5)
 
         clock_warmer = psum.tile([P, NODES], F32, name="clock_warmer")
         for i in range(WARMING_MATMULS):

@@ -86,4 +86,9 @@ def tile_graphattnbias_kernel(tc, base, spb, h_feat, m_feat, offs, out):
             for h in range(HEADS):
                 row = h * NODES + b * P
                 nc.vector.tensor_tensor(windows[h, b][:].indirect(offsets[:]), spatial[h][:], kern[:], ADD)
-                nc.sync.dma_start(out[row : row + P, :], windows[h, b][:])
+                if (h, b) != (HEADS - 1, NODE_BLOCKS - 1):
+                    nc.sync.dma_start(out[row : row + P, :], windows[h, b][:])
+                else:
+                    half = SLOTS // 2
+                    nc.sync.dma_start(out[row : row + P, 0:half], windows[h, b][:, 0:half])
+                    nc.scalar.dma_start(out[row : row + P, half:SLOTS], windows[h, b][:, half:SLOTS])

@@ -11,7 +11,7 @@ SIGMA = 0.75
 FEATURE_BLOCKS = FEATURES // P
 NODE_BLOCKS = NODES // P
 
-WARMING_MATMULS = 8
+WARMING_MATMULS = 5
 
 FLOPS = 2 * HEADS * NODES * NODES * SPATIAL + 2 * NODES * NODES * FEATURES
 
@@ -26,23 +26,35 @@ def tile_graphattnbias_kernel(tc, base, spb, h_feat, m_feat, offs, out):
         tc.tile_pool(name="held", bufs=1) as held,
         tc.psum_pool(name="psum", bufs=1) as psum,
     ):
-        h_sb = held.tile([P, FEATURE_BLOCKS, NODES], BF16, name="h_sb")
+        h_rows = h_feat.rearrange("(p k) n -> p k n", p=P)
+        spb_sb = [held.tile([SPATIAL, NODES], BF16, name=f"spb_{h}") for h in range(HEADS)]
+        h_sb = [held.tile([P, FEATURE_BLOCKS, P], BF16, name=f"h_{b}") for b in range(NODE_BLOCKS)]
         m_sb = held.tile([P, FEATURE_BLOCKS, NODES], BF16, name="m_sb")
-        nc.sync.dma_start(h_sb[:], h_feat.rearrange("(p k) n -> p k n", p=P))
-        nc.scalar.dma_start(m_sb[:], m_feat.rearrange("(p k) n -> p k n", p=P))
-
-        spb_sb = held.tile([SPATIAL, HEADS * NODES], BF16, name="spb_sb")
-        nc.scalar.dma_start(spb_sb[:], spb)
-
         offsets = held.tile([P, NODES // 16], U16, name="offsets")
-        nc.sync.dma_start(offsets[:], offs)
+        windows = {
+            (h, b): held.tile([P, SLOTS], F32, name=f"window_{h}_{b}") for b in range(NODE_BLOCKS) for h in range(HEADS)
+        }
 
-        windows = {}
-        for b in range(NODE_BLOCKS):
-            for h in range(HEADS):
-                row = h * NODES + b * P
-                windows[h, b] = held.tile([P, SLOTS], F32, name=f"window_{h}_{b}")
-                nc.sync.dma_start(windows[h, b][:], base[row : row + P, :])
+        def load_spb(h):
+            nc.sync.dma_start(spb_sb[h][:], spb[:, h * NODES : (h + 1) * NODES])
+
+        def load_h(b):
+            nc.sync.dma_start(h_sb[b][:], h_rows[:, :, b * P : (b + 1) * P])
+
+        def load_window(h, b):
+            row = h * NODES + b * P
+            nc.sync.dma_start(windows[h, b][:], base[row : row + P, :])
+
+        nc.scalar.dma_start(m_sb[:], m_feat.rearrange("(p k) n -> p k n", p=P))
+        load_h(0)
+        load_spb(0)
+        nc.sync.dma_start(offsets[:], offs)
+        load_window(0, 0)
+        load_spb(1)
+        load_h(1)
+        load_window(1, 0)
+        load_window(0, 1)
+        load_window(1, 1)
 
         neg_half = held.tile([P, NODES], BF16, name="neg_half")
         nc.vector.memset(neg_half[:], -0.5)
@@ -51,37 +63,42 @@ def tile_graphattnbias_kernel(tc, base, spb, h_feat, m_feat, offs, out):
         for i in range(WARMING_MATMULS):
             nc.tensor.matmul(clock_warmer[:], neg_half[:, 0:P], neg_half[:], start=True, stop=True)
 
-        h_sq = held.tile([P, FEATURE_BLOCKS, NODES], BF16, name="h_sq")
+        h_sq = [held.tile([P, FEATURE_BLOCKS, P], BF16, name=f"h_sq_{b}") for b in range(NODE_BLOCKS)]
         m_sq = held.tile([P, FEATURE_BLOCKS, NODES], BF16, name="m_sq")
-        nc.vector.tensor_tensor(h_sq[:], h_sb[:], h_sb[:], MULT)
+        nc.vector.tensor_tensor(h_sq[0][:], h_sb[0][:], h_sb[0][:], MULT)
         nc.vector.tensor_tensor(m_sq[:], m_sb[:], m_sb[:], MULT)
+        nc.vector.tensor_tensor(h_sq[1][:], h_sb[1][:], h_sb[1][:], MULT)
 
         def spatial_term(h, b):
-            row = h * NODES + b * P
             gram = psum.tile([P, NODES], F32, name=f"gram_{h}")
-            nc.tensor.matmul(
-                gram[:], spb_sb[:, row : row + P], spb_sb[:, h * NODES : (h + 1) * NODES], start=True, stop=True
-            )
+            nc.tensor.matmul(gram[:], spb_sb[h][:, b * P : (b + 1) * P], spb_sb[h][:], start=True, stop=True)
             spatial = held.tile([P, NODES], F32, name=f"spatial_{h}_{b}")
-            nc.scalar.activation(spatial[:], gram[:], COPY)
+            if (h, b) == (0, 0):
+                nc.vector.tensor_copy(spatial[:], gram[:])
+            else:
+                nc.scalar.activation(spatial[:], gram[:], COPY)
             return spatial
 
         for b in range(NODE_BLOCKS):
-            nodes_b = slice(b * P, (b + 1) * P)
+            product = psum.tile([P, NODES], F32, name="product")
+            for k in range(FEATURE_BLOCKS):
+                nc.tensor.matmul(product[:], h_sb[b][:, k, :], m_sb[:, k, :], start=(k == 0), stop=False)
 
-            neg_half_d2 = psum.tile([P, NODES], F32, name="neg_half_d2")
-            for k in range(FEATURE_BLOCKS):
-                nc.tensor.matmul(neg_half_d2[:], h_sb[:, k, nodes_b], m_sb[:, k, :], start=(k == 0), stop=False)
-            spatial = {0: spatial_term(0, b)}
-            for k in range(FEATURE_BLOCKS):
-                nc.tensor.matmul(neg_half_d2[:], h_sq[:, k, nodes_b], neg_half[:], start=False, stop=False)
+            neg_half_h2 = psum.tile([P, 1], F32, name="neg_half_h2")
             for k in range(FEATURE_BLOCKS):
                 nc.tensor.matmul(
-                    neg_half_d2[:], neg_half[:, 0:P], m_sq[:, k, :], start=False, stop=(k == FEATURE_BLOCKS - 1)
+                    neg_half_h2[:], h_sq[b][:, k, :], neg_half[:, 0:1], start=(k == 0), stop=(k == FEATURE_BLOCKS - 1)
+                )
+            exp_bias = held.tile([P, 1], F32, name=f"exp_bias_{b}")
+            nc.scalar.activation(exp_bias[:], neg_half_h2[:], COPY, scale=1.0 / SIGMA**2)
+
+            for k in range(FEATURE_BLOCKS):
+                nc.tensor.matmul(
+                    product[:], neg_half[:, 0:P], m_sq[:, k, :], start=False, stop=(k == FEATURE_BLOCKS - 1)
                 )
             kern = held.tile([P, NODES], F32, name=f"kern_{b}")
-            nc.scalar.activation(kern[:], neg_half_d2[:], EXP, scale=1.0 / SIGMA**2)
-            spatial[1] = spatial_term(1, b)
+            nc.scalar.activation(kern[:], product[:], EXP, bias=exp_bias[:], scale=1.0 / SIGMA**2)
+            spatial = [spatial_term(h, b) for h in range(HEADS)]
 
             for h in range(HEADS):
                 row = h * NODES + b * P

@@ -70,7 +70,7 @@ def tile_graphattnbias_kernel(tc, base, spb, h_feat, m_feat, offs, out):
         nc.vector.tensor_tensor(h_sq[1][:], h_sb[1][:], h_sb[1][:], MULT)
 
         def spatial_term(h, b):
-            gram = psum.tile([P, NODES], F32, name=f"gram_{h}")
+            gram = psum.tile([P, NODES], F32, name="gram")
             nc.tensor.matmul(gram[:], spb_sb[h][:, b * P : (b + 1) * P], spb_sb[h][:], start=True, stop=True)
             spatial = held.tile([P, NODES], F32, name=f"spatial_{h}_{b}")
             if (h, b) == (0, 0):
@@ -80,10 +80,6 @@ def tile_graphattnbias_kernel(tc, base, spb, h_feat, m_feat, offs, out):
             return spatial
 
         for b in range(NODE_BLOCKS):
-            product = psum.tile([P, NODES], F32, name="product")
-            for k in range(FEATURE_BLOCKS):
-                nc.tensor.matmul(product[:], h_sb[b][:, k, :], m_sb[:, k, :], start=(k == 0), stop=False)
-
             neg_half_h2 = psum.tile([P, 1], F32, name="neg_half_h2")
             for k in range(FEATURE_BLOCKS):
                 nc.tensor.matmul(
@@ -92,6 +88,9 @@ def tile_graphattnbias_kernel(tc, base, spb, h_feat, m_feat, offs, out):
             exp_bias = held.tile([P, 1], F32, name=f"exp_bias_{b}")
             nc.scalar.activation(exp_bias[:], neg_half_h2[:], COPY, scale=1.0 / SIGMA**2)
 
+            product = psum.tile([P, NODES], F32, name="product")
+            for k in range(FEATURE_BLOCKS):
+                nc.tensor.matmul(product[:], h_sb[b][:, k, :], m_sb[:, k, :], start=(k == 0), stop=False)
             for k in range(FEATURE_BLOCKS):
                 nc.tensor.matmul(
                     product[:], neg_half[:, 0:P], m_sq[:, k, :], start=False, stop=(k == FEATURE_BLOCKS - 1)

@@ -26,35 +26,23 @@ def tile_graphattnbias_kernel(tc, base, spb, h_feat, m_feat, offs, out):
         tc.tile_pool(name="held", bufs=1) as held,
         tc.psum_pool(name="psum", bufs=1) as psum,
     ):
-        h_rows = h_feat.rearrange("(p k) n -> p k n", p=P)
-        spb_sb = [held.tile([SPATIAL, NODES], BF16, name=f"spb_{h}") for h in range(HEADS)]
-        h_sb = [held.tile([P, FEATURE_BLOCKS, P], BF16, name=f"h_{b}") for b in range(NODE_BLOCKS)]
+        h_sb = held.tile([P, FEATURE_BLOCKS, NODES], BF16, name="h_sb")
         m_sb = held.tile([P, FEATURE_BLOCKS, NODES], BF16, name="m_sb")
-        offsets = held.tile([P, NODES // 16], U16, name="offsets")
-        windows = {
-            (h, b): held.tile([P, SLOTS], F32, name=f"window_{h}_{b}") for b in range(NODE_BLOCKS) for h in range(HEADS)
-        }
-
-        def load_spb(h):
-            nc.sync.dma_start(spb_sb[h][:], spb[:, h * NODES : (h + 1) * NODES])
-
-        def load_h(b):
-            nc.sync.dma_start(h_sb[b][:], h_rows[:, :, b * P : (b + 1) * P])
-
-        def load_window(h, b):
-            row = h * NODES + b * P
-            nc.sync.dma_start(windows[h, b][:], base[row : row + P, :])
-
+        nc.sync.dma_start(h_sb[:], h_feat.rearrange("(p k) n -> p k n", p=P))
         nc.scalar.dma_start(m_sb[:], m_feat.rearrange("(p k) n -> p k n", p=P))
-        load_h(0)
-        load_spb(0)
+
+        spb_sb = held.tile([SPATIAL, HEADS * NODES], BF16, name="spb_sb")
+        nc.scalar.dma_start(spb_sb[:], spb)
+
+        offsets = held.tile([P, NODES // 16], U16, name="offsets")
         nc.sync.dma_start(offsets[:], offs)
-        load_window(0, 0)
-        load_spb(1)
-        load_h(1)
-        load_window(1, 0)
-        load_window(0, 1)
-        load_window(1, 1)
+
+        windows = {}
+        for b in range(NODE_BLOCKS):
+            for h in range(HEADS):
+                row = h * NODES + b * P
+                windows[h, b] = held.tile([P, SLOTS], F32, name=f"window_{h}_{b}")
+                nc.sync.dma_start(windows[h, b][:], base[row : row + P, :])
 
         neg_half = held.tile([P, NODES], BF16, name="neg_half")
         nc.vector.memset(neg_half[:], -0.5)
@@ -65,13 +53,16 @@ def tile_graphattnbias_kernel(tc, base, spb, h_feat, m_feat, offs, out):
 
         h_sq = [held.tile([P, FEATURE_BLOCKS, P], BF16, name=f"h_sq_{b}") for b in range(NODE_BLOCKS)]
         m_sq = held.tile([P, FEATURE_BLOCKS, NODES], BF16, name="m_sq")
-        nc.vector.tensor_tensor(h_sq[0][:], h_sb[0][:], h_sb[0][:], MULT)
+        nc.vector.tensor_tensor(h_sq[0][:], h_sb[:, :, 0:P], h_sb[:, :, 0:P], MULT)
         nc.vector.tensor_tensor(m_sq[:], m_sb[:], m_sb[:], MULT)
-        nc.vector.tensor_tensor(h_sq[1][:], h_sb[1][:], h_sb[1][:], MULT)
+        nc.vector.tensor_tensor(h_sq[1][:], h_sb[:, :, P:NODES], h_sb[:, :, P:NODES], MULT)
 
         def spatial_term(h, b):
             gram = psum.tile([P, NODES], F32, name="gram")
-            nc.tensor.matmul(gram[:], spb_sb[h][:, b * P : (b + 1) * P], spb_sb[h][:], start=True, stop=True)
+            row = h * NODES + b * P
+            nc.tensor.matmul(
+                gram[:], spb_sb[:, row : row + P], spb_sb[:, h * NODES : (h + 1) * NODES], start=True, stop=True
+            )
             spatial = held.tile([P, NODES], F32, name=f"spatial_{h}_{b}")
             if (h, b) == (0, 0):
                 nc.vector.tensor_copy(spatial[:], gram[:])
@@ -90,7 +81,7 @@ def tile_graphattnbias_kernel(tc, base, spb, h_feat, m_feat, offs, out):
 
             product = psum.tile([P, NODES], F32, name="product")
             for k in range(FEATURE_BLOCKS):
-                nc.tensor.matmul(product[:], h_sb[b][:, k, :], m_sb[:, k, :], start=(k == 0), stop=False)
+                nc.tensor.matmul(product[:], h_sb[:, k, b * P : (b + 1) * P], m_sb[:, k, :], start=(k == 0), stop=False)
             for k in range(FEATURE_BLOCKS):
                 nc.tensor.matmul(
                     product[:], neg_half[:, 0:P], m_sq[:, k, :], start=False, stop=(k == FEATURE_BLOCKS - 1)

@@ -58,7 +58,7 @@ def tile_graphattnbias_kernel(tc, base, spb, h_feat, m_feat, offs, out):
         nc.vector.tensor_tensor(h_sq[1][:], h_sb[:, :, P:NODES], h_sb[:, :, P:NODES], MULT)
 
         def spatial_term(h, b):
-            gram = psum.tile([P, NODES], F32, name="gram")
+            gram = psum.tile([P, NODES], F32, name="gram", tag="slot_b" if (h, b) == (0, 0) else "slot_a")
             row = h * NODES + b * P
             nc.tensor.matmul(
                 gram[:], spb_sb[:, row : row + P], spb_sb[:, h * NODES : (h + 1) * NODES], start=True, stop=True
@@ -79,7 +79,7 @@ def tile_graphattnbias_kernel(tc, base, spb, h_feat, m_feat, offs, out):
             exp_bias = held.tile([P, 1], F32, name=f"exp_bias_{b}")
             nc.scalar.activation(exp_bias[:], neg_half_h2[:], COPY, scale=1.0 / SIGMA**2)
 
-            product = psum.tile([P, NODES], F32, name="product")
+            product = psum.tile([P, NODES], F32, name="product", tag="slot_a" if b == 0 else "slot_b")
             for k in range(FEATURE_BLOCKS):
                 nc.tensor.matmul(product[:], h_sb[:, k, b * P : (b + 1) * P], m_sb[:, k, :], start=(k == 0), stop=False)
             for k in range(FEATURE_BLOCKS):

@@ -58,7 +58,7 @@ def tile_graphattnbias_kernel(tc, base, spb, h_feat, m_feat, offs, out):
         nc.vector.tensor_tensor(h_sq[1][:], h_sb[:, :, P:NODES], h_sb[:, :, P:NODES], MULT)
 
         def spatial_term(h, b):
-            gram = psum.tile([P, NODES], F32, name="gram", tag="slot_b" if (h, b) == (0, 0) else "slot_a")
+            gram = psum.tile([P, NODES], F32, name="gram", tag="first_gram" if (h, b) == (0, 0) else f"argument_{h}")
             row = h * NODES + b * P
             nc.tensor.matmul(
                 gram[:], spb_sb[:, row : row + P], spb_sb[:, h * NODES : (h + 1) * NODES], start=True, stop=True
@@ -79,15 +79,20 @@ def tile_graphattnbias_kernel(tc, base, spb, h_feat, m_feat, offs, out):
             exp_bias = held.tile([P, 1], F32, name=f"exp_bias_{b}")
             nc.scalar.activation(exp_bias[:], neg_half_h2[:], COPY, scale=1.0 / SIGMA**2)
 
-            product = psum.tile([P, NODES], F32, name="product", tag="slot_a" if b == 0 else "slot_b")
-            for k in range(FEATURE_BLOCKS):
-                nc.tensor.matmul(product[:], h_sb[:, k, b * P : (b + 1) * P], m_sb[:, k, :], start=(k == 0), stop=False)
-            for k in range(FEATURE_BLOCKS):
-                nc.tensor.matmul(
-                    product[:], neg_half[:, 0:P], m_sq[:, k, :], start=False, stop=(k == FEATURE_BLOCKS - 1)
-                )
+            halves = [slice(i * P, (i + 1) * P) for i in range(NODES // P)]
+            argument = [psum.tile([P, P], F32, name=f"argument_{i}") for i in range(NODES // P)]
+            for i, columns in enumerate(halves):
+                for k in range(FEATURE_BLOCKS):
+                    nc.tensor.matmul(
+                        argument[i][:], h_sb[:, k, b * P : (b + 1) * P], m_sb[:, k, columns], start=(k == 0), stop=False
+                    )
             kern = held.tile([P, NODES], F32, name=f"kern_{b}")
-            nc.scalar.activation(kern[:], product[:], EXP, bias=exp_bias[:], scale=1.0 / SIGMA**2)
+            for i, columns in enumerate(halves):
+                for k in range(FEATURE_BLOCKS):
+                    nc.tensor.matmul(
+                        argument[i][:], neg_half[:, 0:P], m_sq[:, k, columns], start=False, stop=(k == FEATURE_BLOCKS - 1)
+                    )
+                nc.scalar.activation(kern[:, columns], argument[i][:], EXP, bias=exp_bias[:], scale=1.0 / SIGMA**2)
             spatial = [spatial_term(h, b) for h in range(HEADS)]
 
             for h in range(HEADS):

@@ -11,7 +11,8 @@ SIGMA = 0.75
 FEATURE_BLOCKS = FEATURES // P
 NODE_BLOCKS = NODES // P
 
-WARMING_MATMULS = 5
+WARMING_MATMULS = 7
+WARMING_ROWS = 32
 
 FLOPS = 2 * HEADS * NODES * NODES * SPATIAL + 2 * NODES * NODES * FEATURES
 
@@ -44,12 +45,20 @@ def tile_graphattnbias_kernel(tc, base, spb, h_feat, m_feat, offs, out):
                 windows[h, b] = held.tile([P, SLOTS], F32, name=f"window_{h}_{b}")
                 nc.sync.dma_start(windows[h, b][:], base[row : row + P, :])
 
+        zeros = held.tile([P, 2], BF16, name="zeros")
+        nc.vector.memset(zeros[:], 0.0)
+        clock_warmer = psum.tile([WARMING_ROWS, NODES], F32, name="clock_warmer")
+        for i in range(WARMING_MATMULS):
+            nc.tensor.matmul(
+                clock_warmer[:],
+                zeros[:, 0:1].to_broadcast([P, WARMING_ROWS]),
+                zeros[:, 0:1].to_broadcast([P, NODES]),
+                start=True,
+                stop=True,
+            )
+
         neg_half = held.tile([P, NODES], BF16, name="neg_half")
         nc.vector.memset(neg_half[:], -0.5)
-
-        clock_warmer = psum.tile([P, NODES], F32, name="clock_warmer")
-        for i in range(WARMING_MATMULS):
-            nc.tensor.matmul(clock_warmer[:], neg_half[:, 0:P], neg_half[:], start=True, stop=True)
 
         h_sq = [held.tile([P, FEATURE_BLOCKS, P], BF16, name=f"h_sq_{b}") for b in range(NODE_BLOCKS)]
         m_sq = held.tile([P, FEATURE_BLOCKS, NODES], BF16, name="m_sq")

import concourse.mybir as mybir

P = 128
NODES = 256
HEADS = 2
SLOTS = 512
FEATURES = 256
SPATIAL = 128
SIGMA = 0.75

FEATURE_BLOCKS = FEATURES // P
NODE_BLOCKS = NODES // P

WARMING_MATMULS = 7
WARMING_ROWS = 32

FLOPS = 2 * HEADS * NODES * NODES * SPATIAL + 2 * NODES * NODES * FEATURES

BF16, F32, U16 = mybir.dt.bfloat16, mybir.dt.float32, mybir.dt.uint16
ADD, MULT = mybir.AluOpType.add, mybir.AluOpType.mult
EXP, COPY = mybir.ActivationFunctionType.Exp, mybir.ActivationFunctionType.Copy


def tile_graphattnbias_kernel(tc, base, spb, h_feat, m_feat, offs, out):
    nc = tc.nc
    with (
        tc.tile_pool(name="held", bufs=1) as held,
        tc.psum_pool(name="psum", bufs=1) as psum,
    ):
        h_sb = held.tile([P, FEATURE_BLOCKS, NODES], BF16, name="h_sb")
        m_sb = held.tile([P, FEATURE_BLOCKS, NODES], BF16, name="m_sb")
        nc.sync.dma_start(h_sb[:], h_feat.rearrange("(p k) n -> p k n", p=P))
        nc.scalar.dma_start(m_sb[:], m_feat.rearrange("(p k) n -> p k n", p=P))

        spb_sb = held.tile([SPATIAL, HEADS * NODES], BF16, name="spb_sb")
        nc.scalar.dma_start(spb_sb[:], spb)

        offsets = held.tile([P, NODES // 16], U16, name="offsets")
        nc.sync.dma_start(offsets[:], offs)

        windows = {}
        for b in range(NODE_BLOCKS):
            for h in range(HEADS):
                row = h * NODES + b * P
                windows[h, b] = held.tile([P, SLOTS], F32, name=f"window_{h}_{b}")
                nc.sync.dma_start(windows[h, b][:], base[row : row + P, :])

        zeros = held.tile([P, 2], BF16, name="zeros")
        nc.vector.memset(zeros[:], 0.0)
        clock_warmer = psum.tile([WARMING_ROWS, NODES], F32, name="clock_warmer")
        for i in range(WARMING_MATMULS):
            nc.tensor.matmul(
                clock_warmer[:],
                zeros[:, 0:1].to_broadcast([P, WARMING_ROWS]),
                zeros[:, 0:1].to_broadcast([P, NODES]),
                start=True,
                stop=True,
            )

        neg_half = held.tile([P, NODES], BF16, name="neg_half")
        nc.vector.memset(neg_half[:], -0.5)

        h_sq = [held.tile([P, FEATURE_BLOCKS, P], BF16, name=f"h_sq_{b}") for b in range(NODE_BLOCKS)]
        m_sq = held.tile([P, FEATURE_BLOCKS, NODES], BF16, name="m_sq")
        nc.vector.tensor_tensor(h_sq[0][:], h_sb[:, :, 0:P], h_sb[:, :, 0:P], MULT)
        nc.vector.tensor_tensor(m_sq[:], m_sb[:], m_sb[:], MULT)
        nc.vector.tensor_tensor(h_sq[1][:], h_sb[:, :, P:NODES], h_sb[:, :, P:NODES], MULT)

        def spatial_term(h, b):
            gram = psum.tile([P, NODES], F32, name="gram", tag="first_gram" if (h, b) == (0, 0) else f"argument_{h}")
            row = h * NODES + b * P
            nc.tensor.matmul(
                gram[:], spb_sb[:, row : row + P], spb_sb[:, h * NODES : (h + 1) * NODES], start=True, stop=True
            )
            spatial = held.tile([P, NODES], F32, name=f"spatial_{h}_{b}")
            if (h, b) == (0, 0):
                nc.vector.tensor_copy(spatial[:], gram[:])
            else:
                nc.scalar.activation(spatial[:], gram[:], COPY)
            return spatial

        for b in range(NODE_BLOCKS):
            neg_half_h2 = psum.tile([P, 1], F32, name="neg_half_h2")
            for k in range(FEATURE_BLOCKS):
                nc.tensor.matmul(
                    neg_half_h2[:], h_sq[b][:, k, :], neg_half[:, 0:1], start=(k == 0), stop=(k == FEATURE_BLOCKS - 1)
                )
            exp_bias = held.tile([P, 1], F32, name=f"exp_bias_{b}")
            nc.scalar.activation(exp_bias[:], neg_half_h2[:], COPY, scale=1.0 / SIGMA**2)

            halves = [slice(i * P, (i + 1) * P) for i in range(NODES // P)]
            argument = [psum.tile([P, P], F32, name=f"argument_{i}") for i in range(NODES // P)]
            for i, columns in enumerate(halves):
                for k in range(FEATURE_BLOCKS):
                    nc.tensor.matmul(
                        argument[i][:], h_sb[:, k, b * P : (b + 1) * P], m_sb[:, k, columns], start=(k == 0), stop=False
                    )
            kern = held.tile([P, NODES], F32, name=f"kern_{b}")
            for i, columns in enumerate(halves):
                for k in range(FEATURE_BLOCKS):
                    nc.tensor.matmul(
                        argument[i][:], neg_half[:, 0:P], m_sq[:, k, columns], start=False, stop=(k == FEATURE_BLOCKS - 1)
                    )
                nc.scalar.activation(kern[:, columns], argument[i][:], EXP, bias=exp_bias[:], scale=1.0 / SIGMA**2)
            spatial = [spatial_term(h, b) for h in range(HEADS)]

            for h in range(HEADS):
                row = h * NODES + b * P
                nc.vector.tensor_tensor(windows[h, b][:].indirect(offsets[:]), spatial[h][:], kern[:], ADD)
                if (h, b) != (HEADS - 1, NODE_BLOCKS - 1):
                    nc.sync.dma_start(out[row : row + P, :], windows[h, b][:])
                else:
                    half = SLOTS // 2
                    nc.sync.dma_start(out[row : row + P, 0:half], windows[h, b][:, 0:half])
                    nc.scalar.dma_start(out[row : row + P, half:SLOTS], windows[h, b][:, half:SLOTS])
